import numpy as np
import ml_dtypes

BF16 = ml_dtypes.bfloat16


def bf(x):
    return np.asarray(x, np.float32).astype(BF16)


def f32(x):
    return np.asarray(x, np.float32)


def f64(x):
    return np.asarray(x).astype(np.float64)


def striped(idx):
    return np.tile(idx.reshape(-1, 16).T, (8, 1))


D, S, K, L, B, N = 256, 256, 128, 4, 128, 512


def setup_inputs():
    return {"table": f32(0.5 * np.random.standard_normal((D, S))), "cand": f32(0.5 * np.random.standard_normal((D, K))), "u": bf(2.0 * np.random.standard_normal((D, B)) / np.sqrt(D)), "offs": striped(np.random.permutation(np.tile(np.arange(S), 2))[:N])}


def reference(table, cand, u, offs):
    idx = offs[:16].T.reshape(-1)
    t = f64(table)
    e = f64(cand)
    for pos in range(L):
        e = e + t[:, idx[pos * K:(pos + 1) * K]]
    return f64(u).T @ e

@@ -1,0 +1,68 @@
+import concourse.mybir as mybir
+
+F32, BF16, U16 = mybir.dt.float32, mybir.dt.bfloat16, mybir.dt.uint16
+ADD = mybir.AluOpType.add
+
+P = 128
+FEATURES = 256
+WORDS = 256
+CANDIDATES = 128
+DIALOGUES = 128
+ENTRIES = 512
+BLOCKS = FEATURES // P
+PIECE = 2 * CANDIDATES
+PIECES = ENTRIES // PIECE
+PIECE_COLUMNS = PIECE // 16
+
+FLOPS = 2 * FEATURES * DIALOGUES * CANDIDATES
+
+
+def tile_memn2ndialog_kernel(tc, table, cand, u, offs, out):
+    nc = tc.nc
+    with (
+        tc.tile_pool(name="held", bufs=1) as held,
+        tc.psum_pool(name="psum", bufs=1) as psum,
+    ):
+        offsets = held.tile([P, ENTRIES // 16], U16, name="offsets")
+        nc.sync.dma_start(offsets[:], offs)
+
+        windows, sums, states = [], [], []
+        for blk in range(BLOCKS):
+            rows_lo, rows_hi = blk * P, (blk + 1) * P
+
+            window = held.tile([P, WORDS], F32, name=f"window{blk}")
+            nc.sync.dma_start(window[:], table[rows_lo:rows_hi, :])
+            windows.append(window)
+
+            first = held.tile([P, PIECE], F32, name=f"first{blk}")
+            nc.scalar.dma_start(first[:, 0:CANDIDATES], cand[rows_lo:rows_hi, :])
+            nc.vector.memset(first[:, CANDIDATES:PIECE], 0.0)
+            sums.append(first)
+
+        for blk in range(BLOCKS):
+            state = held.tile([P, DIALOGUES], BF16, name=f"state{blk}")
+            nc.scalar.dma_start(state[:], u[blk * P : (blk + 1) * P, :])
+            states.append(state)
+
+        for piece in range(PIECES):
+            piece_offsets = offsets[:, piece * PIECE_COLUMNS : (piece + 1) * PIECE_COLUMNS]
+            for blk in range(BLOCKS):
+                added = held.tile([P, PIECE], F32, name=f"added{piece}_{blk}")
+                nc.vector.tensor_tensor(
+                    added[:], windows[blk][:].indirect(piece_offsets), sums[blk][:], ADD
+                )
+                sums[blk] = added
+
+        scores = psum.tile([DIALOGUES, CANDIDATES], F32, name="scores")
+        for blk in range(BLOCKS):
+            embedded = held.tile([P, CANDIDATES], BF16, name=f"embedded{blk}")
+            nc.vector.tensor_tensor(
+                embedded[:], sums[blk][:, 0:CANDIDATES], sums[blk][:, CANDIDATES:PIECE], ADD
+            )
+            nc.tensor.matmul(
+                scores[:], states[blk][:], embedded[:], start=(blk == 0), stop=(blk == BLOCKS - 1)
+            )
+
+        staged = held.tile([DIALOGUES, CANDIDATES], F32, name="staged")
+        nc.vector.tensor_copy(staged[:], scores[:])
+        nc.sync.dma_start(out, staged[:])

@@ -31,17 +31,17 @@ def tile_memn2ndialog_kernel(tc, table, cand, u, offs, out):
             rows_lo, rows_hi = blk * P, (blk + 1) * P
 
             window = held.tile([P, WORDS], F32, name=f"window{blk}")
-            nc.sync.dma_start(window[:], table[rows_lo:rows_hi, :])
+            nc.scalar.dma_start(window[:], table[rows_lo:rows_hi, :])
             windows.append(window)
 
             first = held.tile([P, PIECE], F32, name=f"first{blk}")
-            nc.scalar.dma_start(first[:, 0:CANDIDATES], cand[rows_lo:rows_hi, :])
+            nc.sync.dma_start(first[:, 0:CANDIDATES], cand[rows_lo:rows_hi, :])
             nc.vector.memset(first[:, CANDIDATES:PIECE], 0.0)
             sums.append(first)
 
         for blk in range(BLOCKS):
             state = held.tile([P, DIALOGUES], BF16, name=f"state{blk}")
-            nc.scalar.dma_start(state[:], u[blk * P : (blk + 1) * P, :])
+            nc.gpsimd.dma_start(state[:], u[blk * P : (blk + 1) * P, :])
             states.append(state)
 
         for piece in range(PIECES):

@@ -26,32 +26,28 @@ def tile_memn2ndialog_kernel(tc, table, cand, u, offs, out):
         offsets = held.tile([P, ENTRIES // 16], U16, name="offsets")
         nc.sync.dma_start(offsets[:], offs)
 
-        windows, sums, states = [], [], []
-        for blk in range(BLOCKS):
-            rows_lo, rows_hi = blk * P, (blk + 1) * P
+        first = held.tile([P, BLOCKS, PIECE], F32, name="first")
+        nc.scalar.dma_start(first[:, :, 0:CANDIDATES], cand.rearrange("(k p) i -> p k i", p=P))
+        nc.gpsimd.memset(first[:, :, CANDIDATES:PIECE], 0.0)
 
+        windows = []
+        for blk, queue in zip(range(BLOCKS), (nc.sync, nc.scalar)):
             window = held.tile([P, WORDS], F32, name=f"window{blk}")
-            nc.scalar.dma_start(window[:], table[rows_lo:rows_hi, :])
+            queue.dma_start(window[:], table[blk * P : (blk + 1) * P, :])
             windows.append(window)
 
-            first = held.tile([P, PIECE], F32, name=f"first{blk}")
-            nc.sync.dma_start(first[:, 0:CANDIDATES], cand[rows_lo:rows_hi, :])
-            nc.vector.memset(first[:, CANDIDATES:PIECE], 0.0)
-            sums.append(first)
+        states = held.tile([P, BLOCKS, DIALOGUES], BF16, name="states")
+        nc.sync.dma_start(states[:], u.rearrange("(k p) b -> p k b", p=P))
 
-        for blk in range(BLOCKS):
-            state = held.tile([P, DIALOGUES], BF16, name=f"state{blk}")
-            nc.gpsimd.dma_start(state[:], u[blk * P : (blk + 1) * P, :])
-            states.append(state)
-
+        sums = [first[:, blk, :] for blk in range(BLOCKS)]
         for piece in range(PIECES):
             piece_offsets = offsets[:, piece * PIECE_COLUMNS : (piece + 1) * PIECE_COLUMNS]
             for blk in range(BLOCKS):
                 added = held.tile([P, PIECE], F32, name=f"added{piece}_{blk}")
                 nc.vector.tensor_tensor(
-                    added[:], windows[blk][:].indirect(piece_offsets), sums[blk][:], ADD
+                    added[:], windows[blk][:].indirect(piece_offsets), sums[blk], ADD
                 )
-                sums[blk] = added
+                sums[blk] = added[:]
 
         scores = psum.tile([DIALOGUES, CANDIDATES], F32, name="scores")
         for blk in range(BLOCKS):
@@ -60,7 +56,7 @@ def tile_memn2ndialog_kernel(tc, table, cand, u, offs, out):
                 embedded[:], sums[blk][:, 0:CANDIDATES], sums[blk][:, CANDIDATES:PIECE], ADD
             )
             nc.tensor.matmul(
-                scores[:], states[blk][:], embedded[:], start=(blk == 0), stop=(blk == BLOCKS - 1)
+                scores[:], states[:, blk, :], embedded[:], start=(blk == 0), stop=(blk == BLOCKS - 1)
             )
 
         staged = held.tile([DIALOGUES, CANDIDATES], F32, name="staged")

@@ -14,6 +14,9 @@ PIECE = 2 * CANDIDATES
 PIECES = ENTRIES // PIECE
 PIECE_COLUMNS = PIECE // 16
 
+SHARES = 4
+SHARE = CANDIDATES // SHARES
+
 FLOPS = 2 * FEATURES * DIALOGUES * CANDIDATES
 
 
@@ -49,16 +52,22 @@ def tile_memn2ndialog_kernel(tc, table, cand, u, offs, out):
                 )
                 sums[blk] = added[:]
 
-        scores = psum.tile([DIALOGUES, CANDIDATES], F32, name="scores")
+        shares = [slice(s * SHARE, (s + 1) * SHARE) for s in range(SHARES)]
+        scores = [psum.tile([DIALOGUES, SHARE], F32, name=f"scores{s}") for s in range(SHARES)]
+        staged = held.tile([DIALOGUES, CANDIDATES], F32, name="staged")
         for blk in range(BLOCKS):
             embedded = held.tile([P, CANDIDATES], BF16, name=f"embedded{blk}")
-            nc.vector.tensor_tensor(
-                embedded[:], sums[blk][:, 0:CANDIDATES], sums[blk][:, CANDIDATES:PIECE], ADD
-            )
-            nc.tensor.matmul(
-                scores[:], states[:, blk, :], embedded[:], start=(blk == 0), stop=(blk == BLOCKS - 1)
-            )
-
-        staged = held.tile([DIALOGUES, CANDIDATES], F32, name="staged")
-        nc.vector.tensor_copy(staged[:], scores[:])
+            for s, share in enumerate(shares):
+                nc.vector.tensor_tensor(
+                    embedded[:, share],
+                    sums[blk][:, share],
+                    sums[blk][:, CANDIDATES + s * SHARE : CANDIDATES + (s + 1) * SHARE],
+                    ADD,
+                )
+                nc.tensor.matmul(
+                    scores[s][:], states[:, blk, :], embedded[:, share],
+                    start=(blk == 0), stop=(blk == BLOCKS - 1),
+                )
+        for s, share in enumerate(shares):
+            nc.vector.tensor_copy(staged[:, share], scores[s][:])
         nc.sync.dma_start(out, staged[:])

@@ -57,13 +57,15 @@ def tile_memn2ndialog_kernel(tc, table, cand, u, offs, out):
         staged = held.tile([DIALOGUES, CANDIDATES], F32, name="staged")
         for blk in range(BLOCKS):
             embedded = held.tile([P, CANDIDATES], BF16, name=f"embedded{blk}")
-            for s, share in enumerate(shares):
+            folds = shares if blk == BLOCKS - 1 else [slice(0, CANDIDATES)]
+            for fold in folds:
                 nc.vector.tensor_tensor(
-                    embedded[:, share],
-                    sums[blk][:, share],
-                    sums[blk][:, CANDIDATES + s * SHARE : CANDIDATES + (s + 1) * SHARE],
+                    embedded[:, fold],
+                    sums[blk][:, fold],
+                    sums[blk][:, CANDIDATES + fold.start : CANDIDATES + fold.stop],
                     ADD,
                 )
+            for s, share in enumerate(shares):
                 nc.tensor.matmul(
                     scores[s][:], states[:, blk, :], embedded[:, share],
                     start=(blk == 0), stop=(blk == BLOCKS - 1),

@@ -12,7 +12,6 @@ ENTRIES = 512
 BLOCKS = FEATURES // P
 PIECE = 2 * CANDIDATES
 PIECES = ENTRIES // PIECE
-PIECE_COLUMNS = PIECE // 16
 
 SHARES = 4
 SHARE = CANDIDATES // SHARES
@@ -30,26 +29,32 @@ def tile_memn2ndialog_kernel(tc, table, cand, u, offs, out):
         nc.sync.dma_start(offsets[:], offs)
 
         first = held.tile([P, BLOCKS, PIECE], F32, name="first")
-        nc.scalar.dma_start(first[:, :, 0:CANDIDATES], cand.rearrange("(k p) i -> p k i", p=P))
+        nc.sync.dma_start(first[:, :, 0:CANDIDATES], cand.rearrange("(k p) i -> p k i", p=P))
         nc.gpsimd.memset(first[:, :, CANDIDATES:PIECE], 0.0)
 
         windows = []
-        for blk, queue in zip(range(BLOCKS), (nc.sync, nc.scalar)):
+        for blk in range(BLOCKS):
             window = held.tile([P, WORDS], F32, name=f"window{blk}")
-            queue.dma_start(window[:], table[blk * P : (blk + 1) * P, :])
+            nc.scalar.dma_start(window[:], table[blk * P : (blk + 1) * P, :])
             windows.append(window)
 
         states = held.tile([P, BLOCKS, DIALOGUES], BF16, name="states")
         nc.sync.dma_start(states[:], u.rearrange("(k p) b -> p k b", p=P))
 
+        left, right = slice(0, CANDIDATES), slice(CANDIDATES, PIECE)
         sums = [first[:, blk, :] for blk in range(BLOCKS)]
         for piece in range(PIECES):
-            piece_offsets = offsets[:, piece * PIECE_COLUMNS : (piece + 1) * PIECE_COLUMNS]
             for blk in range(BLOCKS):
                 added = held.tile([P, PIECE], F32, name=f"added{piece}_{blk}")
-                nc.vector.tensor_tensor(
-                    added[:], windows[blk][:].indirect(piece_offsets), sums[blk], ADD
-                )
+                parts = [right, left] if piece == 0 and blk == 0 else [slice(0, PIECE)]
+                for part in parts:
+                    entries = slice(
+                        (piece * PIECE + part.start) // 16, (piece * PIECE + part.stop) // 16
+                    )
+                    nc.vector.tensor_tensor(
+                        added[:, part], windows[blk][:].indirect(offsets[:, entries]),
+                        sums[blk][:, part], ADD,
+                    )
                 sums[blk] = added[:]
 
         shares = [slice(s * SHARE, (s + 1) * SHARE) for s in range(SHARES)]

@@ -28,34 +28,37 @@ def tile_memn2ndialog_kernel(tc, table, cand, u, offs, out):
         offsets = held.tile([P, ENTRIES // 16], U16, name="offsets")
         nc.sync.dma_start(offsets[:], offs)
 
-        first = held.tile([P, BLOCKS, PIECE], F32, name="first")
-        nc.sync.dma_start(first[:, :, 0:CANDIDATES], cand.rearrange("(k p) i -> p k i", p=P))
-        nc.gpsimd.memset(first[:, :, CANDIDATES:PIECE], 0.0)
+        first = held.tile([P, (BLOCKS + 1) * CANDIDATES], F32, name="first")
+        cand_columns = BLOCKS * CANDIDATES
+        nc.sync.dma_start(first[:, 0:cand_columns], cand.rearrange("(p k) i -> p (k i)", k=BLOCKS))
+        nc.gpsimd.memset(first[:, cand_columns:], 0.0)
 
+        table_blocks = table.rearrange("(p k) w -> p k w", k=BLOCKS)
         windows = []
         for blk in range(BLOCKS):
             window = held.tile([P, WORDS], F32, name=f"window{blk}")
-            nc.scalar.dma_start(window[:], table[blk * P : (blk + 1) * P, :])
+            nc.scalar.dma_start(window[:], table_blocks[:, blk, :])
             windows.append(window)
 
         states = held.tile([P, BLOCKS, DIALOGUES], BF16, name="states")
-        nc.sync.dma_start(states[:], u.rearrange("(k p) b -> p k b", p=P))
+        nc.sync.dma_start(states[:], u.rearrange("(p k) b -> p k b", k=BLOCKS))
 
-        left, right = slice(0, CANDIDATES), slice(CANDIDATES, PIECE)
-        sums = [first[:, blk, :] for blk in range(BLOCKS)]
-        for piece in range(PIECES):
+        def add_looked_up(out, blk, start, onto):
+            entries = offsets[:, start // 16 : (start + onto.shape[1]) // 16]
+            nc.vector.tensor_tensor(out, windows[blk][:].indirect(entries), onto, ADD)
+
+        zeros = first[:, cand_columns:]
+        added = [
+            [held.tile([P, PIECE], F32, name=f"added{piece}_{blk}") for blk in range(BLOCKS)]
+            for piece in range(PIECES)
+        ]
+        add_looked_up(added[0][0][:, CANDIDATES:PIECE], 0, CANDIDATES, zeros)
+        add_looked_up(added[0][0][:, 0:CANDIDATES], 0, 0, first[:, 0:CANDIDATES])
+        add_looked_up(added[0][1][:], 1, 0, first[:, CANDIDATES:])
+        for piece in range(1, PIECES):
             for blk in range(BLOCKS):
-                added = held.tile([P, PIECE], F32, name=f"added{piece}_{blk}")
-                parts = [right, left] if piece == 0 and blk == 0 else [slice(0, PIECE)]
-                for part in parts:
-                    entries = slice(
-                        (piece * PIECE + part.start) // 16, (piece * PIECE + part.stop) // 16
-                    )
-                    nc.vector.tensor_tensor(
-                        added[:, part], windows[blk][:].indirect(offsets[:, entries]),
-                        sums[blk][:, part], ADD,
-                    )
-                sums[blk] = added[:]
+                add_looked_up(added[piece][blk][:], blk, piece * PIECE, added[piece - 1][blk][:])
+        sums = added[PIECES - 1]
 
         shares = [slice(s * SHARE, (s + 1) * SHARE) for s in range(SHARES)]
         scores = [psum.tile([DIALOGUES, SHARE], F32, name=f"scores{s}") for s in range(SHARES)]

@@ -31,7 +31,7 @@ def tile_memn2ndialog_kernel(tc, table, cand, u, offs, out):
         first = held.tile([P, (BLOCKS + 1) * CANDIDATES], F32, name="first")
         cand_columns = BLOCKS * CANDIDATES
         nc.sync.dma_start(first[:, 0:cand_columns], cand.rearrange("(p k) i -> p (k i)", k=BLOCKS))
-        nc.gpsimd.memset(first[:, cand_columns:], 0.0)
+        nc.vector.memset(first[:, cand_columns:], 0.0)
 
         table_blocks = table.rearrange("(p k) w -> p k w", k=BLOCKS)
         windows = []

@@ -13,8 +13,7 @@ BLOCKS = FEATURES // P
 PIECE = 2 * CANDIDATES
 PIECES = ENTRIES // PIECE
 
-SHARES = 4
-SHARE = CANDIDATES // SHARES
+SHARE_WIDTHS = [eighths * CANDIDATES // 8 for eighths in (2, 3, 3)]
 
 FLOPS = 2 * FEATURES * DIALOGUES * CANDIDATES
 
@@ -60,8 +59,11 @@ def tile_memn2ndialog_kernel(tc, table, cand, u, offs, out):
                 add_looked_up(added[piece][blk][:], blk, piece * PIECE, added[piece - 1][blk][:])
         sums = added[PIECES - 1]
 
-        shares = [slice(s * SHARE, (s + 1) * SHARE) for s in range(SHARES)]
-        scores = [psum.tile([DIALOGUES, SHARE], F32, name=f"scores{s}") for s in range(SHARES)]
+        share_starts = [sum(SHARE_WIDTHS[:s]) for s in range(len(SHARE_WIDTHS))]
+        shares = [slice(a, a + width) for a, width in zip(share_starts, SHARE_WIDTHS)]
+        scores = [
+            psum.tile([DIALOGUES, width], F32, name=f"scores{s}") for s, width in enumerate(SHARE_WIDTHS)
+        ]
         staged = held.tile([DIALOGUES, CANDIDATES], F32, name="staged")
         for blk in range(BLOCKS):
             embedded = held.tile([P, CANDIDATES], BF16, name=f"embedded{blk}")

import concourse.mybir as mybir

F32, BF16, U16 = mybir.dt.float32, mybir.dt.bfloat16, mybir.dt.uint16
ADD = mybir.AluOpType.add

P = 128
FEATURES = 256
WORDS = 256
CANDIDATES = 128
DIALOGUES = 128
ENTRIES = 512
BLOCKS = FEATURES // P
PIECE = 2 * CANDIDATES
PIECES = ENTRIES // PIECE

SHARE_WIDTHS = [eighths * CANDIDATES // 8 for eighths in (2, 3, 3)]

FLOPS = 2 * FEATURES * DIALOGUES * CANDIDATES


def tile_memn2ndialog_kernel(tc, table, cand, u, offs, out):
    nc = tc.nc
    with (
        tc.tile_pool(name="held", bufs=1) as held,
        tc.psum_pool(name="psum", bufs=1) as psum,
    ):
        offsets = held.tile([P, ENTRIES // 16], U16, name="offsets")
        nc.sync.dma_start(offsets[:], offs)

        first = held.tile([P, (BLOCKS + 1) * CANDIDATES], F32, name="first")
        cand_columns = BLOCKS * CANDIDATES
        nc.sync.dma_start(first[:, 0:cand_columns], cand.rearrange("(p k) i -> p (k i)", k=BLOCKS))
        nc.vector.memset(first[:, cand_columns:], 0.0)

        table_blocks = table.rearrange("(p k) w -> p k w", k=BLOCKS)
        windows = []
        for blk in range(BLOCKS):
            window = held.tile([P, WORDS], F32, name=f"window{blk}")
            nc.scalar.dma_start(window[:], table_blocks[:, blk, :])
            windows.append(window)

        states = held.tile([P, BLOCKS, DIALOGUES], BF16, name="states")
        nc.sync.dma_start(states[:], u.rearrange("(p k) b -> p k b", k=BLOCKS))

        def add_looked_up(out, blk, start, onto):
            entries = offsets[:, start // 16 : (start + onto.shape[1]) // 16]
            nc.vector.tensor_tensor(out, windows[blk][:].indirect(entries), onto, ADD)

        zeros = first[:, cand_columns:]
        added = [
            [held.tile([P, PIECE], F32, name=f"added{piece}_{blk}") for blk in range(BLOCKS)]
            for piece in range(PIECES)
        ]
        add_looked_up(added[0][0][:, CANDIDATES:PIECE], 0, CANDIDATES, zeros)
        add_looked_up(added[0][0][:, 0:CANDIDATES], 0, 0, first[:, 0:CANDIDATES])
        add_looked_up(added[0][1][:], 1, 0, first[:, CANDIDATES:])
        for piece in range(1, PIECES):
            for blk in range(BLOCKS):
                add_looked_up(added[piece][blk][:], blk, piece * PIECE, added[piece - 1][blk][:])
        sums = added[PIECES - 1]

        share_starts = [sum(SHARE_WIDTHS[:s]) for s in range(len(SHARE_WIDTHS))]
        shares = [slice(a, a + width) for a, width in zip(share_starts, SHARE_WIDTHS)]
        scores = [
            psum.tile([DIALOGUES, width], F32, name=f"scores{s}") for s, width in enumerate(SHARE_WIDTHS)
        ]
        staged = held.tile([DIALOGUES, CANDIDATES], F32, name="staged")
        for blk in range(BLOCKS):
            embedded = held.tile([P, CANDIDATES], BF16, name=f"embedded{blk}")
            folds = shares if blk == BLOCKS - 1 else [slice(0, CANDIDATES)]
            for fold in folds:
                nc.vector.tensor_tensor(
                    embedded[:, fold],
                    sums[blk][:, fold],
                    sums[blk][:, CANDIDATES + fold.start : CANDIDATES + fold.stop],
                    ADD,
                )
            for s, share in enumerate(shares):
                nc.tensor.matmul(
                    scores[s][:], states[:, blk, :], embedded[:, share],
                    start=(blk == 0), stop=(blk == BLOCKS - 1),
                )
        for s, share in enumerate(shares):
            nc.vector.tensor_copy(staged[:, share], scores[s][:])
        nc.sync.dma_start(out, staged[:])
